import numpy as np
import ml_dtypes


def mxq(x, axis, fmt="e4m3"):
    dtype, down = {"e4m3": (ml_dtypes.float8_e4m3fn, 7), "e5m2": (ml_dtypes.float8_e5m2, 14)}[fmt]
    v = np.moveaxis(np.asarray(x, np.float32).astype(ml_dtypes.bfloat16).astype(np.float64), axis, -1)
    blocks = v.reshape(v.shape[:-1] + (-1, 32))
    amax = np.abs(blocks).max(-1, keepdims=True)
    byte = np.maximum(np.where(amax > 0, np.frexp(amax)[1] - 1 + 127, 0) - down, 1)
    scale = np.exp2(byte - 127.0)
    codes = (blocks / scale).astype(np.float32).astype(dtype).astype(np.float64)
    return np.moveaxis((codes * scale).reshape(v.shape), -1, axis)


WIDE = False


def mx_kscale(k):
    if not WIDE:
        return np.ones(k)
    levels = np.array([10, -10, 5, -5, 0])
    if k % 512:
        return np.exp2(np.random.permutation(np.resize(levels, k // 32))).repeat(32)
    a = np.empty((k // 512, 16))
    for p in range(k // 512):
        a[p, :8] = np.random.permutation(np.resize(levels, 8))
        for g in range(8):
            far = levels[np.abs(levels - a[p, g]) >= 10]
            a[p, g + 8] = far[np.random.randint(len(far))]
    return np.exp2(a.ravel()).repeat(32)


BF16 = ml_dtypes.bfloat16


def bf(x):
    return np.asarray(x, np.float32).astype(BF16)


def f64(x):
    return np.asarray(x).astype(np.float64)


B, N, D, H = 512, 17, 1024, 32
D2 = D // 2
D4 = D // 4
EPS = 1e-5


def layernorm(z, g, b):
    mu = z.mean(-1, keepdims=True)
    var = z.var(-1, keepdims=True)
    return (z - mu) / np.sqrt(var + EPS) * g + b


def setup_inputs():
    s, t = mx_kscale(D), mx_kscale(D2)
    r = np.random.standard_normal
    return {"query": bf(r((B, N, D)) * s),
            "A1W": bf(r((D, D2)) / np.sqrt(D) / s[:, None]),
            "A1b": bf(r(D2) * 0.2),
            "g1": bf((1.0 + 0.1 * r(D2)) * t),
            "b1": bf(r(D2) * 0.2 * t),
            "A2W": bf(r((D2, D4)) / np.sqrt(D2) / t[:, None]),
            "A2b": bf(r(D4) * 0.2),
            "g2": bf(1.0 + 0.1 * r(D4)),
            "b2": bf(r(D4) * 0.2)}


def reference(query, A1W, A1b, g1, b1, A2W, A2b, g2, b2):
    u = (mxq(f64(query), 2, "e4m3") @ mxq(f64(A1W), 0, "e4m3")) + f64(A1b)
    j1 = np.maximum(layernorm(u, f64(g1), f64(b1)), 0.0)
    w = (mxq(j1, 2, "e4m3") @ mxq(f64(A2W), 0, "e4m3")) + f64(A2b)
    return np.maximum(layernorm(w, f64(g2), f64(b2)), 0.0)

@@ -1,0 +1,374 @@
+from contextlib import ExitStack
+
+import concourse.mybir as mybir
+from concourse.masks import make_identity
+
+F32 = mybir.dt.float32
+BF16 = mybir.dt.bfloat16
+U32 = mybir.dt.uint32
+U8 = mybir.dt.uint8
+FP8X4 = mybir.dt.float8_e4m3fn_x4
+ALU = mybir.AluOpType
+ACT = mybir.ActivationFunctionType
+
+P = 128
+PACK = 4
+ROWS = 512 * 17
+D = 1024
+D2 = 512
+D4 = 256
+EPS = 1e-5
+TILES = 4
+BLOCK = TILES * P
+BLOCKS = ROWS // BLOCK
+PASSES = D // (P * PACK)
+
+FLOPS = 2 * ROWS * (D * D2 + D2 * D4)
+
+Q_COPY = 0
+LOAD = 3
+Q_QUANTISE = 4
+U_BIAS = 6
+U_STATS = 10
+U_RSTD = 11
+U_NORMALISE = 12
+J1_PLANE = 17
+J1_GROUP = 22
+J1_QUANTISE = 23
+W_BIAS = 25
+W_STATS = 29
+W_RSTD = 30
+W_GAIN = 30
+W_SHIFT = 31
+O_STORE = 35
+
+
+def quantise_weight(nc, pool, raw, codes, scales, width, strands):
+    grouped = pool.tile([P, width, PACK], BF16, align_bytes=64, name="grouped", tag="grouped%d" % width)
+    nc.vector.tensor_copy(
+        out=grouped[:].rearrange("p (s m) t -> p s m t", s=strands),
+        in_=raw.rearrange("p t (m s) -> p s m t", s=strands),
+    )
+    nc.vector.quantize_mx(
+        out=codes.bitcast(FP8X4), scales=scales, in_=grouped[:].rearrange("p n t -> p (n t)")
+    )
+
+
+def tile_multiheadedattention_pa_t_kernel(tc, query, A1W, A1b, g1, b1, A2W, A2b, g2, b2, out):
+    nc = tc.nc
+    q_rows = query.flatten_outer_dims()
+    out_rows = out.flatten_outer_dims()
+
+    with ExitStack() as ctx:
+        const = ctx.enter_context(tc.tile_pool(name="const", bufs=1))
+        two = ctx.enter_context(tc.tile_pool(name="two", bufs=2))
+        three = ctx.enter_context(tc.tile_pool(name="three", bufs=3))
+        small = ctx.enter_context(tc.tile_pool(name="small", bufs=4))
+        psum = ctx.enter_context(tc.psum_pool(name="psum", bufs=2))
+
+        held = {}
+
+        def block_rows(b):
+            return slice(b * BLOCK, (b + 1) * BLOCK)
+
+        def load(b):
+            q_sb = three.tile([P, TILES * D], BF16, name="q_sb")
+            nc.sync.dma_start(out=q_sb[:], in_=q_rows[block_rows(b), :].rearrange("(p j) k -> p (j k)", j=TILES))
+            held["q_sb", b] = q_sb
+
+        def q_transpose(b, j):
+            q_words = held["q_sb", b][:].bitcast(F32)
+            qT = psum.tile([P, D2], F32, name="qT")
+            for h in range(D2 // P):
+                col = j * D2 + (h // 2) * 2 * P + h % 2
+                nc.tensor.transpose(qT[:, h * P : (h + 1) * P], q_words[:, col : col + 2 * P - 1 : 2], ident[:])
+            held["qT", b, j] = qT
+
+        def q_copy(b, j):
+            if j == 0:
+                held["qg", b] = two.tile([P, TILES * D], BF16, align_bytes=64, name="qg")
+            qg_words = held["qg", b][:].bitcast(F32)
+            nc.scalar.copy(
+                out=qg_words[:, j * D2 : (j + 1) * D2].rearrange("p (g r u) -> p g r u", g=PASSES, u=2),
+                in_=held["qT", b, j][:].rearrange("p (g u r) -> p g r u", g=PASSES, u=2),
+            )
+
+        def q_quantise(b):
+            q_codes = two.tile([P, TILES * PASSES * P], U32, align_bytes=64, name="q_codes")
+            q_scales = two.tile([P, TILES * PASSES * P], U8, align_bytes=64, name="q_scales")
+            nc.vector.quantize_mx(out=q_codes[:].bitcast(FP8X4), scales=q_scales[:], in_=held["qg", b][:])
+            held["q_codes", b] = q_codes
+            held["q_scales", b] = q_scales
+
+        def u_matmul(b, j):
+            mm1 = psum.tile([P, D2], F32, name="mm1")
+            for g in range(PASSES):
+                cols = slice((j * PASSES + g) * P, (j * PASSES + g + 1) * P)
+                nc.tensor.matmul_mx(
+                    out=mm1[:],
+                    lhsT=held["q_codes", b][:, cols].bitcast(FP8X4),
+                    lhsT_scale=held["q_scales", b][:, cols],
+                    rhs=a1_codes[:, g, :].bitcast(FP8X4),
+                    rhs_scale=a1_scales[:, g, :],
+                    start=(g == 0),
+                    stop=(g == PASSES - 1),
+                )
+            held["mm1", b, j] = mm1
+
+        def u_bias(b, j):
+            if j == 0:
+                held["u", b] = three.tile([P, TILES, D2], F32, name="u_sb")
+                held["u_sum", b] = small.tile([P, TILES], F32, name="u_sum")
+            nc.vector.scalar_tensor_tensor(
+                out=held["u", b][:, j, :],
+                in0=held["mm1", b, j][:],
+                scalar=1.0,
+                in1=a1b_all[:],
+                op0=ALU.mult,
+                op1=ALU.add,
+                accum_out=held["u_sum", b][:, j : j + 1],
+            )
+
+        def u_squares(b, j):
+            if j == 0:
+                held["u_sq", b] = two.tile([P, TILES, D2], BF16, name="u_sq")
+                held["u_ssq", b] = small.tile([P, TILES], F32, name="u_ssq")
+            nc.scalar.activation(
+                out=held["u_sq", b][:, j, :],
+                in_=held["u", b][:, j, :],
+                func=ACT.Square,
+                bias=held["u_sum", b][:, j : j + 1],
+                scale=-1.0 * D2,
+                accum_out=held["u_ssq", b][:, j : j + 1],
+            )
+
+        def u_stats(b):
+            u_std = small.tile([P, TILES], F32, name="u_std")
+            nc.scalar.activation(
+                out=u_std[:], in_=held["u_ssq", b][:], func=ACT.Sqrt, bias=eps[:, 0:1], scale=1.0 / (D2 * D2 * D2)
+            )
+            u_negmean = small.tile([P, TILES], F32, name="u_negmean")
+            nc.gpsimd.tensor_scalar(
+                out=u_negmean[:], in0=held["u_sum", b][:], scalar1=-1.0 / D2, scalar2=0.0, op0=ALU.mult, op1=ALU.add
+            )
+            held["u_std", b] = u_std
+            held["u_negmean", b] = u_negmean
+
+        def u_rstd(b):
+            held["u_rstd", b] = small.tile([P, TILES], F32, name="u_rstd")
+            nc.vector.reciprocal(out=held["u_rstd", b][:], in_=held["u_std", b][:])
+
+        def u_normalise(b, j):
+            if j == 0:
+                held["y", b] = two.tile([P, TILES, D2], F32, name="y_sb")
+            nc.vector.tensor_scalar(
+                out=held["y", b][:, j, :],
+                in0=held["u", b][:, j, :],
+                scalar1=held["u_negmean", b][:, j : j + 1],
+                scalar2=held["u_rstd", b][:, j : j + 1],
+                op0=ALU.add,
+                op1=ALU.mult,
+            )
+
+        def y_transpose(b, t):
+            yT = psum.tile([P, BLOCK], F32, name="yT")
+            for j in range(TILES):
+                nc.tensor.transpose(yT[:, j * P : (j + 1) * P], held["y", b][:, j, t * P : (t + 1) * P], ident[:])
+            held["yT", b, t] = yT
+
+        def j1_plane(b, t):
+            if t == 0:
+                held["j1_planes", b] = two.tile([P, PACK, BLOCK], BF16, name="j1_planes")
+            nc.scalar.activation(
+                out=held["j1_planes", b][:, t, :],
+                in_=held["yT", b, t][:],
+                func=ACT.Relu,
+                bias=gb_cols[:, PACK + t : PACK + t + 1],
+                scale=gb_cols[:, t : t + 1],
+            )
+
+        def j1_group(b):
+            j1_grouped = two.tile([P, BLOCK, PACK], BF16, align_bytes=64, name="j1_grouped")
+            nc.vector.tensor_copy(
+                out=j1_grouped[:].rearrange("p (c i) t -> p c t i", i=4),
+                in_=held["j1_planes", b][:].rearrange("p t (c i) -> p c t i", i=4),
+            )
+            held["j1_grouped", b] = j1_grouped
+
+        def j1_quantise(b):
+            j1_codes = two.tile([P, BLOCK], U32, align_bytes=64, name="j1_codes")
+            j1_scales = two.tile([P, BLOCK], U8, align_bytes=64, name="j1_scales")
+            nc.vector.quantize_mx(
+                out=j1_codes[:].bitcast(FP8X4),
+                scales=j1_scales[:],
+                in_=held["j1_grouped", b][:].rearrange("p r t -> p (r t)"),
+            )
+            held["j1_codes", b] = j1_codes
+            held["j1_scales", b] = j1_scales
+
+        def w_matmul(b, j):
+            mm2 = psum.tile([P, D4], F32, name="mm2")
+            nc.tensor.matmul_mx(
+                out=mm2[:],
+                lhsT=held["j1_codes", b][:, j * P : (j + 1) * P].bitcast(FP8X4),
+                lhsT_scale=held["j1_scales", b][:, j * P : (j + 1) * P],
+                rhs=a2_codes[:].bitcast(FP8X4),
+                rhs_scale=a2_scales[:],
+                start=True,
+                stop=True,
+            )
+            held["mm2", b, j] = mm2
+
+        def w_bias(b, j):
+            if j == 0:
+                held["w", b] = three.tile([P, TILES, D4], F32, name="w_sb")
+                held["w_sum", b] = small.tile([P, TILES], F32, name="w_sum")
+            nc.vector.scalar_tensor_tensor(
+                out=held["w", b][:, j, :],
+                in0=held["mm2", b, j][:],
+                scalar=1.0,
+                in1=a2b_all[:],
+                op0=ALU.mult,
+                op1=ALU.add,
+                accum_out=held["w_sum", b][:, j : j + 1],
+            )
+
+        def w_squares(b, j):
+            if j == 0:
+                held["w_sq", b] = two.tile([P, TILES, D4], BF16, name="w_sq")
+                held["w_ssq", b] = small.tile([P, TILES], F32, name="w_ssq")
+            nc.scalar.activation(
+                out=held["w_sq", b][:, j, :],
+                in_=held["w", b][:, j, :],
+                func=ACT.Square,
+                bias=held["w_sum", b][:, j : j + 1],
+                scale=-1.0 * D4,
+                accum_out=held["w_ssq", b][:, j : j + 1],
+            )
+
+        def w_stats(b):
+            w_std = small.tile([P, TILES], F32, name="w_std")
+            nc.scalar.activation(
+                out=w_std[:], in_=held["w_ssq", b][:], func=ACT.Sqrt, bias=eps[:, 0:1], scale=1.0 / (D4 * D4 * D4)
+            )
+            w_negmean = small.tile([P, TILES], F32, name="w_negmean")
+            nc.gpsimd.tensor_scalar(
+                out=w_negmean[:], in0=held["w_sum", b][:], scalar1=-1.0 / D4, scalar2=0.0, op0=ALU.mult, op1=ALU.add
+            )
+            held["w_std", b] = w_std
+            held["w_negmean", b] = w_negmean
+
+        def w_rstd(b):
+            held["w_rstd", b] = small.tile([P, TILES], F32, name="w_rstd")
+            nc.vector.reciprocal(out=held["w_rstd", b][:], in_=held["w_std", b][:])
+
+        def w_gain(b, j):
+            if j == 0:
+                held["w_gain", b] = two.tile([P, TILES, D4], F32, name="w_gain")
+            nc.vector.scalar_tensor_tensor(
+                out=held["w_gain", b][:, j, :],
+                in0=held["w", b][:, j, :],
+                scalar=held["w_negmean", b][:, j : j + 1],
+                in1=g2_all[:],
+                op0=ALU.add,
+                op1=ALU.mult,
+            )
+
+        def w_shift(b, j):
+            if j == 0:
+                held["o", b] = three.tile([P, TILES, D4], F32, name="o_sb")
+            nc.vector.scalar_tensor_tensor(
+                out=held["o", b][:, j, :],
+                in0=held["w_gain", b][:, j, :],
+                scalar=held["w_rstd", b][:, j : j + 1],
+                in1=b2_all[:],
+                op0=ALU.mult,
+                op1=ALU.add,
+            )
+
+        def o_store(b):
+            o_sb = held["o", b]
+            nc.scalar.activation(out=o_sb[:], in_=o_sb[:], func=ACT.Relu)
+            nc.sync.dma_start(out=out_rows[block_rows(b), :].rearrange("(p j) n -> p j n", j=TILES), in_=o_sb[:])
+
+        load(0)
+        ident = const.tile([P, P], F32)
+        make_identity(nc, ident[:])
+        eps = const.tile([P, 1], F32)
+        nc.vector.memset(eps[:], EPS)
+
+        a1_raw = const.tile([P, PASSES * PACK, D2], BF16)
+        nc.scalar.dma_start(
+            out=a1_raw[:].rearrange("p (g t) n -> p g (t n)", t=PACK),
+            in_=A1W.rearrange("(g p t) n -> p g (t n)", p=P, t=PACK),
+        )
+        a1_codes = const.tile([P, PASSES, D2], U32, align_bytes=64)
+        a1_scales = const.tile([P, PASSES, D2], U8, align_bytes=64)
+        for g in range(PASSES):
+            quantise_weight(
+                nc, const, a1_raw[:, g * PACK : (g + 1) * PACK, :], a1_codes[:, g, :], a1_scales[:, g, :], D2, PACK
+            )
+
+        a1b_raw = const.tile([P, D2], BF16)
+        nc.scalar.dma_start(out=a1b_raw[:], in_=A1b.partition_broadcast(P))
+        a1b_all = const.tile([P, D2], BF16)
+        nc.vector.tensor_copy(
+            out=a1b_all[:].rearrange("p (s m) -> p s m", s=PACK), in_=a1b_raw[:].rearrange("p (m s) -> p s m", s=PACK)
+        )
+
+        g1_raw = const.tile([P, PACK], BF16)
+        nc.scalar.dma_start(out=g1_raw[:], in_=g1.rearrange("(p t) -> p t", t=PACK))
+        b1_raw = const.tile([P, PACK], BF16)
+        nc.scalar.dma_start(out=b1_raw[:], in_=b1.rearrange("(p t) -> p t", t=PACK))
+        gb_cols = const.tile([P, 2 * PACK], F32)
+        nc.vector.tensor_copy(out=gb_cols[:, 0:PACK], in_=g1_raw[:])
+        nc.vector.tensor_copy(out=gb_cols[:, PACK : 2 * PACK], in_=b1_raw[:])
+
+        a2_raw = const.tile([P, PACK, D4], BF16)
+        nc.scalar.dma_start(out=a2_raw[:], in_=A2W.rearrange("(p t) n -> p t n", t=PACK))
+        a2_codes = const.tile([P, D4], U32, align_bytes=64)
+        a2_scales = const.tile([P, D4], U8, align_bytes=64)
+        quantise_weight(nc, const, a2_raw[:], a2_codes[:], a2_scales[:], D4, 1)
+        a2b_all = const.tile([P, D4], BF16)
+        nc.scalar.dma_start(out=a2b_all[:], in_=A2b.partition_broadcast(P))
+        g2_all = const.tile([P, D4], BF16)
+        nc.scalar.dma_start(out=g2_all[:], in_=g2.partition_broadcast(P))
+        b2_all = const.tile([P, D4], BF16)
+        nc.scalar.dma_start(out=b2_all[:], in_=b2.partition_broadcast(P))
+
+        load(1)
+        load(2)
+
+        def for_tile(stage, n):
+            if 0 <= n < BLOCKS * TILES:
+                stage(n // TILES, n % TILES)
+
+        def for_block(stage, n, ahead=0):
+            if n % TILES == 0 and 0 <= n // TILES + ahead < BLOCKS and n >= 0:
+                stage(n // TILES + ahead)
+
+        with tc.manual_schedule():
+            for step in range(-1, BLOCKS * TILES + O_STORE + 1):
+                for_tile(q_transpose, step + 1 - Q_COPY)
+                for_tile(y_transpose, step + 1 - J1_PLANE)
+                for_tile(u_matmul, step + 1 - U_BIAS)
+                for_tile(w_matmul, step + 1 - W_BIAS)
+
+                for_tile(u_bias, step - U_BIAS)
+                for_tile(q_copy, step - Q_COPY)
+                for_tile(u_normalise, step - U_NORMALISE)
+                for_tile(j1_plane, step - J1_PLANE)
+                for_tile(w_bias, step - W_BIAS)
+                for_tile(u_squares, step - U_BIAS)
+                for_block(u_stats, step - U_STATS)
+                for_tile(w_gain, step - W_GAIN)
+                for_tile(w_shift, step - W_SHIFT)
+                for_tile(w_squares, step - W_BIAS)
+                for_block(w_stats, step - W_STATS)
+                for_block(q_quantise, step - Q_QUANTISE)
+                for_block(j1_group, step - J1_GROUP)
+                for_block(j1_quantise, step - J1_QUANTISE)
+                for_block(u_rstd, step - U_RSTD)
+                for_block(w_rstd, step - W_RSTD)
+                for_block(o_store, step - O_STORE)
+                for_block(load, step - LOAD, ahead=3)

@@ -27,20 +27,21 @@ FLOPS = 2 * ROWS * (D * D2 + D2 * D4)
 
 Q_COPY = 0
 LOAD = 3
-Q_QUANTISE = 4
-U_BIAS = 6
-U_STATS = 10
-U_RSTD = 11
-U_NORMALISE = 12
-J1_PLANE = 17
-J1_GROUP = 22
-J1_QUANTISE = 23
-W_BIAS = 25
-W_STATS = 29
-W_RSTD = 30
-W_GAIN = 30
-W_SHIFT = 31
-O_STORE = 35
+Q_QUANTISE = 1
+U_BIAS = 3
+U_STATS = 7
+U_RSTD = 7
+U_NORMALISE = 8
+J1_PLANE = 13
+J1_GROUP = 17
+J1_QUANTISE = 18
+W_BIAS = 20
+W_STATS = 24
+W_RSTD = 24
+W_GAIN = 25
+W_SHIFT = 26
+O_RELU = 27
+O_STORE = 30
 
 
 def quantise_weight(nc, pool, raw, codes, scales, width, strands):
@@ -76,6 +77,14 @@ def tile_multiheadedattention_pa_t_kernel(tc, query, A1W, A1b, g1, b1, A2W, A2b,
             nc.sync.dma_start(out=q_sb[:], in_=q_rows[block_rows(b), :].rearrange("(p j) k -> p (j k)", j=TILES))
             held["q_sb", b] = q_sb
 
+        def load_tile(b, j):
+            if j == 0:
+                held["q_sb", b] = three.tile([P, TILES * D], BF16, name="q_sb")
+            nc.sync.dma_start(
+                out=held["q_sb", b][:, j * D : (j + 1) * D],
+                in_=q_rows[block_rows(b), :].rearrange("(p j) k -> p j k", j=TILES)[:, j, :],
+            )
+
         def q_transpose(b, j):
             q_words = held["q_sb", b][:].bitcast(F32)
             qT = psum.tile([P, D2], F32, name="qT")
@@ -93,12 +102,16 @@ def tile_multiheadedattention_pa_t_kernel(tc, query, A1W, A1b, g1, b1, A2W, A2b,
                 in_=held["qT", b, j][:].rearrange("p (g u r) -> p g r u", g=PASSES, u=2),
             )
 
-        def q_quantise(b):
-            q_codes = two.tile([P, TILES * PASSES * P], U32, align_bytes=64, name="q_codes")
-            q_scales = two.tile([P, TILES * PASSES * P], U8, align_bytes=64, name="q_scales")
-            nc.vector.quantize_mx(out=q_codes[:].bitcast(FP8X4), scales=q_scales[:], in_=held["qg", b][:])
-            held["q_codes", b] = q_codes
-            held["q_scales", b] = q_scales
+        def q_quantise(b, j):
+            if j == 0:
+                held["q_codes", b] = two.tile([P, TILES * PASSES * P], U32, align_bytes=64, name="q_codes")
+                held["q_scales", b] = two.tile([P, TILES * PASSES * P], U8, align_bytes=64, name="q_scales")
+            cols = slice(j * PASSES * P, (j + 1) * PASSES * P)
+            nc.vector.quantize_mx(
+                out=held["q_codes", b][:, cols].bitcast(FP8X4),
+                scales=held["q_scales", b][:, cols],
+                in_=held["qg", b][:, j * D : (j + 1) * D],
+            )
 
         def u_matmul(b, j):
             mm1 = psum.tile([P, D2], F32, name="mm1")
@@ -187,24 +200,25 @@ def tile_multiheadedattention_pa_t_kernel(tc, query, A1W, A1b, g1, b1, A2W, A2b,
                 scale=gb_cols[:, t : t + 1],
             )
 
-        def j1_group(b):
-            j1_grouped = two.tile([P, BLOCK, PACK], BF16, align_bytes=64, name="j1_grouped")
+        def j1_group(b, j):
+            if j == 0:
+                held["j1_grouped", b] = two.tile([P, BLOCK, PACK], BF16, align_bytes=64, name="j1_grouped")
+            rows = slice(j * P, (j + 1) * P)
             nc.vector.tensor_copy(
-                out=j1_grouped[:].rearrange("p (c i) t -> p c t i", i=4),
-                in_=held["j1_planes", b][:].rearrange("p t (c i) -> p c t i", i=4),
+                out=held["j1_grouped", b][:, rows, :].rearrange("p (c i) t -> p c t i", i=4),
+                in_=held["j1_planes", b][:, :, rows].rearrange("p t (c i) -> p c t i", i=4),
             )
-            held["j1_grouped", b] = j1_grouped
 
-        def j1_quantise(b):
-            j1_codes = two.tile([P, BLOCK], U32, align_bytes=64, name="j1_codes")
-            j1_scales = two.tile([P, BLOCK], U8, align_bytes=64, name="j1_scales")
+        def j1_quantise(b, j):
+            if j == 0:
+                held["j1_codes", b] = two.tile([P, BLOCK], U32, align_bytes=64, name="j1_codes")
+                held["j1_scales", b] = two.tile([P, BLOCK], U8, align_bytes=64, name="j1_scales")
+            rows = slice(j * P, (j + 1) * P)
             nc.vector.quantize_mx(
-                out=j1_codes[:].bitcast(FP8X4),
-                scales=j1_scales[:],
-                in_=held["j1_grouped", b][:].rearrange("p r t -> p (r t)"),
+                out=held["j1_codes", b][:, rows].bitcast(FP8X4),
+                scales=held["j1_scales", b][:, rows],
+                in_=held["j1_grouped", b][:, rows, :].rearrange("p r t -> p (r t)"),
             )
-            held["j1_codes", b] = j1_codes
-            held["j1_scales", b] = j1_scales
 
         def w_matmul(b, j):
             mm2 = psum.tile([P, D4], F32, name="mm2")
@@ -286,58 +300,64 @@ def tile_multiheadedattention_pa_t_kernel(tc, query, A1W, A1b, g1, b1, A2W, A2b,
                 op1=ALU.add,
             )
 
+        def o_relu(b, j):
+            o_tile = held["o", b][:, j, :]
+            nc.scalar.activation(out=o_tile, in_=o_tile, func=ACT.Relu)
+
         def o_store(b):
             o_sb = held["o", b]
-            nc.scalar.activation(out=o_sb[:], in_=o_sb[:], func=ACT.Relu)
             nc.sync.dma_start(out=out_rows[block_rows(b), :].rearrange("(p j) n -> p j n", j=TILES), in_=o_sb[:])
 
-        load(0)
-        ident = const.tile([P, P], F32)
-        make_identity(nc, ident[:])
+        load_tile(0, 0)
+        load_tile(0, 1)
+        a1_raw = const.tile([P, PASSES, PACK, D2], BF16)
+        for g in range(PASSES):
+            nc.sync.dma_start(
+                out=a1_raw[:, g, :, :],
+                in_=A1W[g * P * PACK : (g + 1) * P * PACK, :].rearrange("(p t) n -> p t n", t=PACK),
+            )
+            load_tile(0, 2 + g)
+        a1b_raw = const.tile([P, D2], BF16)
+        nc.sync.dma_start(out=a1b_raw[:], in_=A1b.partition_broadcast(P))
+        load(1)
+        g1_raw = const.tile([P, PACK], BF16)
+        nc.sync.dma_start(out=g1_raw[:], in_=g1.rearrange("(p t) -> p t", t=PACK))
+        b1_raw = const.tile([P, PACK], BF16)
+        nc.sync.dma_start(out=b1_raw[:], in_=b1.rearrange("(p t) -> p t", t=PACK))
+        a2_raw = const.tile([P, PACK, D4], BF16)
+        nc.sync.dma_start(out=a2_raw[:], in_=A2W.rearrange("(p t) n -> p t n", t=PACK))
+        load(2)
+        a2b_all = const.tile([P, D4], BF16)
+        nc.sync.dma_start(out=a2b_all[:], in_=A2b.partition_broadcast(P))
+        g2_all = const.tile([P, D4], BF16)
+        nc.sync.dma_start(out=g2_all[:], in_=g2.partition_broadcast(P))
+        b2_all = const.tile([P, D4], BF16)
+        nc.sync.dma_start(out=b2_all[:], in_=b2.partition_broadcast(P))
+
         eps = const.tile([P, 1], F32)
         nc.vector.memset(eps[:], EPS)
+        warm = const.tile([P, 1], F32)
+        nc.scalar.activation(out=warm[:], in_=eps[:], func=ACT.Sqrt)
+        ident = const.tile([P, P], F32)
+        make_identity(nc, ident[:])
 
-        a1_raw = const.tile([P, PASSES * PACK, D2], BF16)
-        nc.scalar.dma_start(
-            out=a1_raw[:].rearrange("p (g t) n -> p g (t n)", t=PACK),
-            in_=A1W.rearrange("(g p t) n -> p g (t n)", p=P, t=PACK),
-        )
         a1_codes = const.tile([P, PASSES, D2], U32, align_bytes=64)
         a1_scales = const.tile([P, PASSES, D2], U8, align_bytes=64)
         for g in range(PASSES):
-            quantise_weight(
-                nc, const, a1_raw[:, g * PACK : (g + 1) * PACK, :], a1_codes[:, g, :], a1_scales[:, g, :], D2, PACK
-            )
+            quantise_weight(nc, const, a1_raw[:, g, :, :], a1_codes[:, g, :], a1_scales[:, g, :], D2, PACK)
 
-        a1b_raw = const.tile([P, D2], BF16)
-        nc.scalar.dma_start(out=a1b_raw[:], in_=A1b.partition_broadcast(P))
         a1b_all = const.tile([P, D2], BF16)
         nc.vector.tensor_copy(
             out=a1b_all[:].rearrange("p (s m) -> p s m", s=PACK), in_=a1b_raw[:].rearrange("p (m s) -> p s m", s=PACK)
         )
 
-        g1_raw = const.tile([P, PACK], BF16)
-        nc.scalar.dma_start(out=g1_raw[:], in_=g1.rearrange("(p t) -> p t", t=PACK))
-        b1_raw = const.tile([P, PACK], BF16)
-        nc.scalar.dma_start(out=b1_raw[:], in_=b1.rearrange("(p t) -> p t", t=PACK))
         gb_cols = const.tile([P, 2 * PACK], F32)
         nc.vector.tensor_copy(out=gb_cols[:, 0:PACK], in_=g1_raw[:])
         nc.vector.tensor_copy(out=gb_cols[:, PACK : 2 * PACK], in_=b1_raw[:])
 
-        a2_raw = const.tile([P, PACK, D4], BF16)
-        nc.scalar.dma_start(out=a2_raw[:], in_=A2W.rearrange("(p t) n -> p t n", t=PACK))
         a2_codes = const.tile([P, D4], U32, align_bytes=64)
         a2_scales = const.tile([P, D4], U8, align_bytes=64)
         quantise_weight(nc, const, a2_raw[:], a2_codes[:], a2_scales[:], D4, 1)
-        a2b_all = const.tile([P, D4], BF16)
-        nc.scalar.dma_start(out=a2b_all[:], in_=A2b.partition_broadcast(P))
-        g2_all = const.tile([P, D4], BF16)
-        nc.scalar.dma_start(out=g2_all[:], in_=g2.partition_broadcast(P))
-        b2_all = const.tile([P, D4], BF16)
-        nc.scalar.dma_start(out=b2_all[:], in_=b2.partition_broadcast(P))
-
-        load(1)
-        load(2)
 
         def for_tile(stage, n):
             if 0 <= n < BLOCKS * TILES:
@@ -355,19 +375,20 @@ def tile_multiheadedattention_pa_t_kernel(tc, query, A1W, A1b, g1, b1, A2W, A2b,
                 for_tile(w_matmul, step + 1 - W_BIAS)
 
                 for_tile(u_bias, step - U_BIAS)
-                for_tile(q_copy, step - Q_COPY)
-                for_tile(u_normalise, step - U_NORMALISE)
-                for_tile(j1_plane, step - J1_PLANE)
+                for_tile(j1_quantise, step - J1_QUANTISE)
                 for_tile(w_bias, step - W_BIAS)
-                for_tile(u_squares, step - U_BIAS)
-                for_block(u_stats, step - U_STATS)
+                for_tile(u_normalise, step - U_NORMALISE)
                 for_tile(w_gain, step - W_GAIN)
+                for_tile(q_quantise, step - Q_QUANTISE)
                 for_tile(w_shift, step - W_SHIFT)
-                for_tile(w_squares, step - W_BIAS)
+                for_tile(j1_group, step - J1_GROUP)
+                for_block(u_stats, step - U_STATS)
                 for_block(w_stats, step - W_STATS)
-                for_block(q_quantise, step - Q_QUANTISE)
-                for_block(j1_group, step - J1_GROUP)
-                for_block(j1_quantise, step - J1_QUANTISE)
+                for_tile(q_copy, step - Q_COPY)
+                for_tile(j1_plane, step - J1_PLANE)
+                for_tile(u_squares, step - U_BIAS)
+                for_tile(w_squares, step - W_BIAS)
+                for_tile(o_relu, step - O_RELU)
                 for_block(u_rstd, step - U_RSTD)
                 for_block(w_rstd, step - W_RSTD)
                 for_block(o_store, step - O_STORE)

@@ -171,16 +171,26 @@ def tile_multiheadedattention_pa_t_kernel(tc, query, A1W, A1b, g1, b1, A2W, A2b,
             held["u_rstd", b] = small.tile([P, TILES], F32, name="u_rstd")
             nc.vector.reciprocal(out=held["u_rstd", b][:], in_=held["u_std", b][:])
 
+        def u_offset(b, j):
+            if j == 0:
+                held["u_offset", b] = small.tile([P, TILES], F32, name="u_offset")
+            nc.vector.tensor_tensor(
+                out=held["u_offset", b][:, j : j + 1],
+                in0=held["u_negmean", b][:, j : j + 1],
+                in1=held["u_rstd", b][:, j : j + 1],
+                op=ALU.mult,
+            )
+
         def u_normalise(b, j):
             if j == 0:
                 held["y", b] = two.tile([P, TILES, D2], F32, name="y_sb")
-            nc.vector.tensor_scalar(
+            nc.gpsimd.tensor_scalar(
                 out=held["y", b][:, j, :],
                 in0=held["u", b][:, j, :],
-                scalar1=held["u_negmean", b][:, j : j + 1],
-                scalar2=held["u_rstd", b][:, j : j + 1],
-                op0=ALU.add,
-                op1=ALU.mult,
+                scalar1=held["u_rstd", b][:, j : j + 1],
+                scalar2=held["u_offset", b][:, j : j + 1],
+                op0=ALU.mult,
+                op1=ALU.add,
             )
 
         def y_transpose(b, t):
@@ -374,22 +384,23 @@ def tile_multiheadedattention_pa_t_kernel(tc, query, A1W, A1b, g1, b1, A2W, A2b,
                 for_tile(u_matmul, step + 1 - U_BIAS)
                 for_tile(w_matmul, step + 1 - W_BIAS)
 
-                for_tile(u_bias, step - U_BIAS)
-                for_tile(j1_quantise, step - J1_QUANTISE)
-                for_tile(w_bias, step - W_BIAS)
+                for_block(u_stats, step - U_STATS)
+                for_block(w_stats, step - W_STATS)
+                for_tile(u_offset, step - U_NORMALISE)
                 for_tile(u_normalise, step - U_NORMALISE)
+                for_tile(u_bias, step - U_BIAS)
+                for_tile(w_bias, step - W_BIAS)
+                for_tile(j1_quantise, step - J1_QUANTISE)
                 for_tile(w_gain, step - W_GAIN)
                 for_tile(q_quantise, step - Q_QUANTISE)
                 for_tile(w_shift, step - W_SHIFT)
+                for_block(u_rstd, step - U_RSTD)
+                for_block(w_rstd, step - W_RSTD)
                 for_tile(j1_group, step - J1_GROUP)
-                for_block(u_stats, step - U_STATS)
-                for_block(w_stats, step - W_STATS)
                 for_tile(q_copy, step - Q_COPY)
                 for_tile(j1_plane, step - J1_PLANE)
                 for_tile(u_squares, step - U_BIAS)
                 for_tile(w_squares, step - W_BIAS)
                 for_tile(o_relu, step - O_RELU)
-                for_block(u_rstd, step - U_RSTD)
-                for_block(w_rstd, step - W_RSTD)
                 for_block(o_store, step - O_STORE)
                 for_block(load, step - LOAD, ahead=3)

@@ -18,41 +18,44 @@ D = 1024
 D2 = 512
 D4 = 256
 EPS = 1e-5
-TILES = 4
-BLOCK = TILES * P
-BLOCKS = ROWS // BLOCK
 PASSES = D // (P * PACK)
+AHEAD = 3
+
+SIZES = [4] * 17
+FIRST = [sum(SIZES[:b]) for b in range(len(SIZES))]
 
 FLOPS = 2 * ROWS * (D * D2 + D2 * D4)
 
-Q_COPY = 0
-LOAD = 3
-Q_QUANTISE = 1
-U_BIAS = 3
-U_STATS = 7
-U_RSTD = 7
-U_NORMALISE = 8
-J1_PLANE = 13
-J1_GROUP = 17
-J1_QUANTISE = 18
-W_BIAS = 20
-W_STATS = 24
-W_RSTD = 24
-W_GAIN = 25
-W_SHIFT = 26
-O_RELU = 27
-O_STORE = 30
+LAG = {
+    "load": (1, -1),
+    "q_copy": (0, 0),
+    "q_quantise": (0, 1),
+    "u_bias": (0, 3),
+    "u_stats": (1, 3),
+    "u_normalise": (1, 4),
+    "j1_plane": (2, 5),
+    "j1_group": (3, 5),
+    "j1_quantise": (3, 6),
+    "w_bias": (3, 7),
+    "w_stats": (4, 7),
+    "w_gain": (4, 8),
+    "w_shift": (4, 9),
+    "o_relu": (4, 10),
+    "o_store": (5, 9),
+}
+BLOCK_STAGES = ("load", "u_stats", "w_stats", "o_store")
+LATER_CONSTANTS = 5
 
 
-def quantise_weight(nc, pool, raw, codes, scales, width, strands):
-    grouped = pool.tile([P, width, PACK], BF16, align_bytes=64, name="grouped", tag="grouped%d" % width)
+def group_weight(nc, grouped, raw, strands):
     nc.vector.tensor_copy(
-        out=grouped[:].rearrange("p (s m) t -> p s m t", s=strands),
+        out=grouped.rearrange("p (s m) t -> p s m t", s=strands),
         in_=raw.rearrange("p t (m s) -> p s m t", s=strands),
     )
-    nc.vector.quantize_mx(
-        out=codes.bitcast(FP8X4), scales=scales, in_=grouped[:].rearrange("p n t -> p (n t)")
-    )
+
+
+def quantise_weight(nc, codes, scales, grouped):
+    nc.vector.quantize_mx(out=codes.bitcast(FP8X4), scales=scales, in_=grouped.rearrange("p n t -> p (n t)"))
 
 
 def tile_multiheadedattention_pa_t_kernel(tc, query, A1W, A1b, g1, b1, A2W, A2b, g2, b2, out):
@@ -64,63 +67,60 @@ def tile_multiheadedattention_pa_t_kernel(tc, query, A1W, A1b, g1, b1, A2W, A2b,
         const = ctx.enter_context(tc.tile_pool(name="const", bufs=1))
         two = ctx.enter_context(tc.tile_pool(name="two", bufs=2))
         three = ctx.enter_context(tc.tile_pool(name="three", bufs=3))
-        small = ctx.enter_context(tc.tile_pool(name="small", bufs=4))
+        small = ctx.enter_context(tc.tile_pool(name="small", bufs=6))
+        deep = ctx.enter_context(tc.tile_pool(name="deep", bufs=12))
         psum = ctx.enter_context(tc.psum_pool(name="psum", bufs=2))
 
         held = {}
 
         def block_rows(b):
-            return slice(b * BLOCK, (b + 1) * BLOCK)
+            return slice(FIRST[b] * P, (FIRST[b] + SIZES[b]) * P)
 
         def load(b):
-            q_sb = three.tile([P, TILES * D], BF16, name="q_sb")
-            nc.sync.dma_start(out=q_sb[:], in_=q_rows[block_rows(b), :].rearrange("(p j) k -> p (j k)", j=TILES))
+            q_sb = three.tile([P, SIZES[b], D], BF16, name="q_sb")
+            nc.sync.dma_start(out=q_sb[:], in_=q_rows[block_rows(b), :].rearrange("(p j) k -> p j k", j=SIZES[b]))
             held["q_sb", b] = q_sb
 
         def load_tile(b, j):
             if j == 0:
-                held["q_sb", b] = three.tile([P, TILES * D], BF16, name="q_sb")
+                held["q_sb", b] = three.tile([P, SIZES[b], D], BF16, name="q_sb")
             nc.sync.dma_start(
-                out=held["q_sb", b][:, j * D : (j + 1) * D],
-                in_=q_rows[block_rows(b), :].rearrange("(p j) k -> p j k", j=TILES)[:, j, :],
+                out=held["q_sb", b][:, j, :],
+                in_=q_rows[block_rows(b), :].rearrange("(p j) k -> p j k", j=SIZES[b])[:, j, :],
             )
 
         def q_transpose(b, j):
-            q_words = held["q_sb", b][:].bitcast(F32)
-            qT = psum.tile([P, D2], F32, name="qT")
-            for h in range(D2 // P):
-                col = j * D2 + (h // 2) * 2 * P + h % 2
-                nc.tensor.transpose(qT[:, h * P : (h + 1) * P], q_words[:, col : col + 2 * P - 1 : 2], ident[:])
+            q_words = held["q_sb", b][:, j, :].bitcast(F32)
+            qT = psum.tile([P, PASSES, 2, P], F32, name="qT")
+            for g in range(PASSES):
+                for u in range(2):
+                    col = g * 2 * P + u
+                    nc.tensor.transpose(qT[:, g, u, :], q_words[:, col : col + 2 * P - 1 : 2], ident[:])
             held["qT", b, j] = qT
 
         def q_copy(b, j):
-            if j == 0:
-                held["qg", b] = two.tile([P, TILES * D], BF16, align_bytes=64, name="qg")
-            qg_words = held["qg", b][:].bitcast(F32)
+            qg = three.tile([P, D], BF16, align_bytes=64, name="qg")
             nc.scalar.copy(
-                out=qg_words[:, j * D2 : (j + 1) * D2].rearrange("p (g r u) -> p g r u", g=PASSES, u=2),
-                in_=held["qT", b, j][:].rearrange("p (g u r) -> p g r u", g=PASSES, u=2),
+                out=qg[:].bitcast(F32).rearrange("p (g r u) -> p g r u", g=PASSES, u=2),
+                in_=held["qT", b, j][:].rearrange("p g u r -> p g r u"),
             )
+            held["qg", b, j] = qg
 
         def q_quantise(b, j):
-            if j == 0:
-                held["q_codes", b] = two.tile([P, TILES * PASSES * P], U32, align_bytes=64, name="q_codes")
-                held["q_scales", b] = two.tile([P, TILES * PASSES * P], U8, align_bytes=64, name="q_scales")
-            cols = slice(j * PASSES * P, (j + 1) * PASSES * P)
-            nc.vector.quantize_mx(
-                out=held["q_codes", b][:, cols].bitcast(FP8X4),
-                scales=held["q_scales", b][:, cols],
-                in_=held["qg", b][:, j * D : (j + 1) * D],
-            )
+            q_codes = three.tile([P, PASSES * P], U32, align_bytes=64, name="q_codes")
+            q_scales = three.tile([P, PASSES * P], U8, align_bytes=64, name="q_scales")
+            nc.vector.quantize_mx(out=q_codes[:].bitcast(FP8X4), scales=q_scales[:], in_=held["qg", b, j][:])
+            held["q_codes", b, j] = q_codes
+            held["q_scales", b, j] = q_scales
 
         def u_matmul(b, j):
             mm1 = psum.tile([P, D2], F32, name="mm1")
             for g in range(PASSES):
-                cols = slice((j * PASSES + g) * P, (j * PASSES + g + 1) * P)
+                cols = slice(g * P, (g + 1) * P)
                 nc.tensor.matmul_mx(
                     out=mm1[:],
-                    lhsT=held["q_codes", b][:, cols].bitcast(FP8X4),
-                    lhsT_scale=held["q_scales", b][:, cols],
+                    lhsT=held["q_codes", b, j][:, cols].bitcast(FP8X4),
+                    lhsT_scale=held["q_scales", b, j][:, cols],
                     rhs=a1_codes[:, g, :].bitcast(FP8X4),
                     rhs_scale=a1_scales[:, g, :],
                     start=(g == 0),
@@ -130,10 +130,10 @@ def tile_multiheadedattention_pa_t_kernel(tc, query, A1W, A1b, g1, b1, A2W, A2b,
 
         def u_bias(b, j):
             if j == 0:
-                held["u", b] = three.tile([P, TILES, D2], F32, name="u_sb")
-                held["u_sum", b] = small.tile([P, TILES], F32, name="u_sum")
+                held["u_sum", b] = small.tile([P, SIZES[b]], F32, name="u_sum")
+            u_sb = deep.tile([P, D2], F32, name="u_sb")
             nc.vector.scalar_tensor_tensor(
-                out=held["u", b][:, j, :],
+                out=u_sb[:],
                 in0=held["mm1", b, j][:],
                 scalar=1.0,
                 in1=a1b_all[:],
@@ -141,14 +141,15 @@ def tile_multiheadedattention_pa_t_kernel(tc, query, A1W, A1b, g1, b1, A2W, A2b,
                 op1=ALU.add,
                 accum_out=held["u_sum", b][:, j : j + 1],
             )
+            held["u", b, j] = u_sb
 
         def u_squares(b, j):
             if j == 0:
-                held["u_sq", b] = two.tile([P, TILES, D2], BF16, name="u_sq")
-                held["u_ssq", b] = small.tile([P, TILES], F32, name="u_ssq")
+                held["u_ssq", b] = small.tile([P, SIZES[b]], F32, name="u_ssq")
+            u_sq = two.tile([P, D2], BF16, name="u_sq")
             nc.scalar.activation(
-                out=held["u_sq", b][:, j, :],
-                in_=held["u", b][:, j, :],
+                out=u_sq[:],
+                in_=held["u", b, j][:],
                 func=ACT.Square,
                 bias=held["u_sum", b][:, j : j + 1],
                 scale=-1.0 * D2,
@@ -156,86 +157,89 @@ def tile_multiheadedattention_pa_t_kernel(tc, query, A1W, A1b, g1, b1, A2W, A2b,
             )
 
         def u_stats(b):
-            u_std = small.tile([P, TILES], F32, name="u_std")
+            held["u_rstd", b] = small.tile([P, SIZES[b]], F32, name="u_rstd")
             nc.scalar.activation(
-                out=u_std[:], in_=held["u_ssq", b][:], func=ACT.Sqrt, bias=eps[:, 0:1], scale=1.0 / (D2 * D2 * D2)
+                out=held["u_rstd", b][:],
+                in_=held["u_ssq", b][:],
+                func=ACT.Abs_reciprocal_sqrt,
+                bias=eps[:, 0:1],
+                scale=1.0 / (D2 * D2 * D2),
             )
-            u_negmean = small.tile([P, TILES], F32, name="u_negmean")
-            nc.gpsimd.tensor_scalar(
-                out=u_negmean[:], in0=held["u_sum", b][:], scalar1=-1.0 / D2, scalar2=0.0, op0=ALU.mult, op1=ALU.add
-            )
-            held["u_std", b] = u_std
-            held["u_negmean", b] = u_negmean
-
-        def u_rstd(b):
-            held["u_rstd", b] = small.tile([P, TILES], F32, name="u_rstd")
-            nc.vector.reciprocal(out=held["u_rstd", b][:], in_=held["u_std", b][:])
 
         def u_offset(b, j):
             if j == 0:
-                held["u_offset", b] = small.tile([P, TILES], F32, name="u_offset")
-            nc.vector.tensor_tensor(
+                held["u_offset", b] = small.tile([P, SIZES[b]], F32, name="u_offset")
+            nc.vector.scalar_tensor_tensor(
                 out=held["u_offset", b][:, j : j + 1],
-                in0=held["u_negmean", b][:, j : j + 1],
+                in0=held["u_sum", b][:, j : j + 1],
+                scalar=-1.0 / D2,
                 in1=held["u_rstd", b][:, j : j + 1],
-                op=ALU.mult,
+                op0=ALU.mult,
+                op1=ALU.mult,
             )
 
         def u_normalise(b, j):
-            if j == 0:
-                held["y", b] = two.tile([P, TILES, D2], F32, name="y_sb")
+            y_sb = deep.tile([P, D2], F32, name="y_sb")
             nc.gpsimd.tensor_scalar(
-                out=held["y", b][:, j, :],
-                in0=held["u", b][:, j, :],
+                out=y_sb[:],
+                in0=held["u", b, j][:],
                 scalar1=held["u_rstd", b][:, j : j + 1],
                 scalar2=held["u_offset", b][:, j : j + 1],
                 op0=ALU.mult,
                 op1=ALU.add,
             )
+            held["y", b, j] = y_sb
 
-        def y_transpose(b, t):
-            yT = psum.tile([P, BLOCK], F32, name="yT")
-            for j in range(TILES):
-                nc.tensor.transpose(yT[:, j * P : (j + 1) * P], held["y", b][:, j, t * P : (t + 1) * P], ident[:])
-            held["yT", b, t] = yT
+        def planes(b, i):
+            turn = PACK // SIZES[b]
+            return range(i * turn, (i + 1) * turn)
 
-        def j1_plane(b, t):
-            if t == 0:
-                held["j1_planes", b] = two.tile([P, PACK, BLOCK], BF16, name="j1_planes")
-            nc.scalar.activation(
-                out=held["j1_planes", b][:, t, :],
-                in_=held["yT", b, t][:],
-                func=ACT.Relu,
-                bias=gb_cols[:, PACK + t : PACK + t + 1],
-                scale=gb_cols[:, t : t + 1],
-            )
+        def y_transpose(b, i):
+            yT = psum.tile([P, D2], F32, name="yT")
+            for n, t in enumerate(planes(b, i)):
+                for j in range(SIZES[b]):
+                    at = (n * SIZES[b] + j) * P
+                    nc.tensor.transpose(yT[:, at : at + P], held["y", b, j][:, t * P : (t + 1) * P], ident[:])
+            held["yT", b, i] = yT
+
+        def j1_plane(b, i):
+            width = SIZES[b] * P
+            if i == 0:
+                held["j1_planes", b] = three.tile([P, PACK, width], BF16, name="j1_planes")
+            for n, t in enumerate(planes(b, i)):
+                nc.scalar.activation(
+                    out=held["j1_planes", b][:, t, :],
+                    in_=held["yT", b, i][:, n * width : (n + 1) * width],
+                    func=ACT.Relu,
+                    bias=gb_cols[:, PACK + t : PACK + t + 1],
+                    scale=gb_cols[:, t : t + 1],
+                )
 
         def j1_group(b, j):
-            if j == 0:
-                held["j1_grouped", b] = two.tile([P, BLOCK, PACK], BF16, align_bytes=64, name="j1_grouped")
-            rows = slice(j * P, (j + 1) * P)
-            nc.vector.tensor_copy(
-                out=held["j1_grouped", b][:, rows, :].rearrange("p (c i) t -> p c t i", i=4),
-                in_=held["j1_planes", b][:, :, rows].rearrange("p t (c i) -> p c t i", i=4),
+            j1_grouped = three.tile([P, P, PACK], BF16, align_bytes=64, name="j1_grouped")
+            (nc.scalar.copy if (j == 3 and b % 2) or (j % 2 == 1 and b >= 13) else nc.vector.tensor_copy)(
+                out=j1_grouped[:].rearrange("p (c i) t -> p c t i", i=4),
+                in_=held["j1_planes", b][:, :, j * P : (j + 1) * P].rearrange("p t (c i) -> p c t i", i=4),
             )
+            held["j1_grouped", b, j] = j1_grouped
 
         def j1_quantise(b, j):
-            if j == 0:
-                held["j1_codes", b] = two.tile([P, BLOCK], U32, align_bytes=64, name="j1_codes")
-                held["j1_scales", b] = two.tile([P, BLOCK], U8, align_bytes=64, name="j1_scales")
-            rows = slice(j * P, (j + 1) * P)
+            j1_codes = three.tile([P, P], U32, align_bytes=64, name="j1_codes")
+            j1_scales = three.tile([P, P], U8, align_bytes=64, name="j1_scales")
             nc.vector.quantize_mx(
-                out=held["j1_codes", b][:, rows].bitcast(FP8X4),
-                scales=held["j1_scales", b][:, rows],
-                in_=held["j1_grouped", b][:, rows, :].rearrange("p r t -> p (r t)"),
+                out=j1_codes[:].bitcast(FP8X4),
+                scales=j1_scales[:],
+                in_=held["j1_grouped", b, j][:].rearrange("p r t -> p (r t)"),
             )
+            held["j1_codes", b, j] = j1_codes
+            held["j1_scales", b, j] = j1_scales
 
         def w_matmul(b, j):
             mm2 = psum.tile([P, D4], F32, name="mm2")
             nc.tensor.matmul_mx(
                 out=mm2[:],
-                lhsT=held["j1_codes", b][:, j * P : (j + 1) * P].bitcast(FP8X4),
-                lhsT_scale=held["j1_scales", b][:, j * P : (j + 1) * P],
+                lhsT=held["j1_codes", b, j][:].bitcast(FP8X4),
+                lhsT_scale=held["j1_scales", b, j][:],
                 rhs=a2_codes[:].bitcast(FP8X4),
                 rhs_scale=a2_scales[:],
                 start=True,
@@ -245,10 +249,10 @@ def tile_multiheadedattention_pa_t_kernel(tc, query, A1W, A1b, g1, b1, A2W, A2b,
 
         def w_bias(b, j):
             if j == 0:
-                held["w", b] = three.tile([P, TILES, D4], F32, name="w_sb")
-                held["w_sum", b] = small.tile([P, TILES], F32, name="w_sum")
+                held["w_sum", b] = small.tile([P, SIZES[b]], F32, name="w_sum")
+            w_sb = deep.tile([P, D4], F32, name="w_sb")
             nc.vector.scalar_tensor_tensor(
-                out=held["w", b][:, j, :],
+                out=w_sb[:],
                 in0=held["mm2", b, j][:],
                 scalar=1.0,
                 in1=a2b_all[:],
@@ -256,14 +260,15 @@ def tile_multiheadedattention_pa_t_kernel(tc, query, A1W, A1b, g1, b1, A2W, A2b,
                 op1=ALU.add,
                 accum_out=held["w_sum", b][:, j : j + 1],
             )
+            held["w", b, j] = w_sb
 
         def w_squares(b, j):
             if j == 0:
-                held["w_sq", b] = two.tile([P, TILES, D4], BF16, name="w_sq")
-                held["w_ssq", b] = small.tile([P, TILES], F32, name="w_ssq")
+                held["w_ssq", b] = small.tile([P, SIZES[b]], F32, name="w_ssq")
+            w_sq = two.tile([P, D4], BF16, name="w_sq")
             nc.scalar.activation(
-                out=held["w_sq", b][:, j, :],
-                in_=held["w", b][:, j, :],
+                out=w_sq[:],
+                in_=held["w", b, j][:],
                 func=ACT.Square,
                 bias=held["w_sum", b][:, j : j + 1],
                 scale=-1.0 * D4,
@@ -271,39 +276,42 @@ def tile_multiheadedattention_pa_t_kernel(tc, query, A1W, A1b, g1, b1, A2W, A2b,
             )
 
         def w_stats(b):
-            w_std = small.tile([P, TILES], F32, name="w_std")
+            held["w_rstd", b] = small.tile([P, SIZES[b]], F32, name="w_rstd")
             nc.scalar.activation(
-                out=w_std[:], in_=held["w_ssq", b][:], func=ACT.Sqrt, bias=eps[:, 0:1], scale=1.0 / (D4 * D4 * D4)
+                out=held["w_rstd", b][:],
+                in_=held["w_ssq", b][:],
+                func=ACT.Abs_reciprocal_sqrt,
+                bias=eps[:, 0:1],
+                scale=1.0 / (D4 * D4 * D4),
             )
-            w_negmean = small.tile([P, TILES], F32, name="w_negmean")
+            held["w_negmean", b] = small.tile([P, SIZES[b]], F32, name="w_negmean")
             nc.gpsimd.tensor_scalar(
-                out=w_negmean[:], in0=held["w_sum", b][:], scalar1=-1.0 / D4, scalar2=0.0, op0=ALU.mult, op1=ALU.add
+                out=held["w_negmean", b][:],
+                in0=held["w_sum", b][:],
+                scalar1=-1.0 / D4,
+                scalar2=0.0,
+                op0=ALU.mult,
+                op1=ALU.add,
             )
-            held["w_std", b] = w_std
-            held["w_negmean", b] = w_negmean
-
-        def w_rstd(b):
-            held["w_rstd", b] = small.tile([P, TILES], F32, name="w_rstd")
-            nc.vector.reciprocal(out=held["w_rstd", b][:], in_=held["w_std", b][:])
 
         def w_gain(b, j):
-            if j == 0:
-                held["w_gain", b] = two.tile([P, TILES, D4], F32, name="w_gain")
+            w_gain_sb = three.tile([P, D4], F32, name="w_gain_sb")
             nc.vector.scalar_tensor_tensor(
-                out=held["w_gain", b][:, j, :],
-                in0=held["w", b][:, j, :],
+                out=w_gain_sb[:],
+                in0=held["w", b, j][:],
                 scalar=held["w_negmean", b][:, j : j + 1],
                 in1=g2_all[:],
                 op0=ALU.add,
                 op1=ALU.mult,
             )
+            held["w_gain", b, j] = w_gain_sb
 
         def w_shift(b, j):
             if j == 0:
-                held["o", b] = three.tile([P, TILES, D4], F32, name="o_sb")
+                held["o", b] = three.tile([P, SIZES[b], D4], F32, name="o_sb")
             nc.vector.scalar_tensor_tensor(
                 out=held["o", b][:, j, :],
-                in0=held["w_gain", b][:, j, :],
+                in0=held["w_gain", b, j][:],
                 scalar=held["w_rstd", b][:, j : j + 1],
                 in1=b2_all[:],
                 op0=ALU.mult,
@@ -315,18 +323,18 @@ def tile_multiheadedattention_pa_t_kernel(tc, query, A1W, A1b, g1, b1, A2W, A2b,
             nc.scalar.activation(out=o_tile, in_=o_tile, func=ACT.Relu)
 
         def o_store(b):
-            o_sb = held["o", b]
-            nc.sync.dma_start(out=out_rows[block_rows(b), :].rearrange("(p j) n -> p j n", j=TILES), in_=o_sb[:])
+            nc.sync.dma_start(
+                out=out_rows[block_rows(b), :].rearrange("(p j) n -> p j n", j=SIZES[b]), in_=held["o", b][:]
+            )
 
-        load_tile(0, 0)
-        load_tile(0, 1)
         a1_raw = const.tile([P, PASSES, PACK, D2], BF16)
         for g in range(PASSES):
             nc.sync.dma_start(
                 out=a1_raw[:, g, :, :],
                 in_=A1W[g * P * PACK : (g + 1) * P * PACK, :].rearrange("(p t) n -> p t n", t=PACK),
             )
-            load_tile(0, 2 + g)
+        for j in range(SIZES[0]):
+            load_tile(0, j)
         a1b_raw = const.tile([P, D2], BF16)
         nc.sync.dma_start(out=a1b_raw[:], in_=A1b.partition_broadcast(P))
         load(1)
@@ -347,14 +355,17 @@ def tile_multiheadedattention_pa_t_kernel(tc, query, A1W, A1b, g1, b1, A2W, A2b,
         eps = const.tile([P, 1], F32)
         nc.vector.memset(eps[:], EPS)
         warm = const.tile([P, 1], F32)
-        nc.scalar.activation(out=warm[:], in_=eps[:], func=ACT.Sqrt)
+        nc.scalar.activation(out=warm[:], in_=eps[:], func=ACT.Abs_reciprocal_sqrt)
         ident = const.tile([P, P], F32)
         make_identity(nc, ident[:])
 
+        a1_grouped = const.tile([P, PASSES, D2, PACK], BF16, align_bytes=64)
         a1_codes = const.tile([P, PASSES, D2], U32, align_bytes=64)
         a1_scales = const.tile([P, PASSES, D2], U8, align_bytes=64)
         for g in range(PASSES):
-            quantise_weight(nc, const, a1_raw[:, g, :, :], a1_codes[:, g, :], a1_scales[:, g, :], D2, PACK)
+            group_weight(nc, a1_grouped[:, g, :, :], a1_raw[:, g, :, :], PACK)
+        for g in range(PASSES):
+            quantise_weight(nc, a1_codes[:, g, :], a1_scales[:, g, :], a1_grouped[:, g, :, :])
 
         a1b_all = const.tile([P, D2], BF16)
         nc.vector.tensor_copy(
@@ -362,45 +373,59 @@ def tile_multiheadedattention_pa_t_kernel(tc, query, A1W, A1b, g1, b1, A2W, A2b,
         )
 
         gb_cols = const.tile([P, 2 * PACK], F32)
-        nc.vector.tensor_copy(out=gb_cols[:, 0:PACK], in_=g1_raw[:])
-        nc.vector.tensor_copy(out=gb_cols[:, PACK : 2 * PACK], in_=b1_raw[:])
-
         a2_codes = const.tile([P, D4], U32, align_bytes=64)
         a2_scales = const.tile([P, D4], U8, align_bytes=64)
-        quantise_weight(nc, const, a2_raw[:], a2_codes[:], a2_scales[:], D4, 1)
+        a2_grouped = const.tile([P, D4, PACK], BF16, align_bytes=64)
 
-        def for_tile(stage, n):
-            if 0 <= n < BLOCKS * TILES:
-                stage(n // TILES, n % TILES)
+        def later_constants():
+            nc.vector.tensor_copy(out=gb_cols[:, 0:PACK], in_=g1_raw[:])
+            nc.vector.tensor_copy(out=gb_cols[:, PACK : 2 * PACK], in_=b1_raw[:])
 
-        def for_block(stage, n, ahead=0):
-            if n % TILES == 0 and 0 <= n // TILES + ahead < BLOCKS and n >= 0:
-                stage(n // TILES + ahead)
+            group_weight(nc, a2_grouped[:], a2_raw[:], 1)
+            quantise_weight(nc, a2_codes[:], a2_scales[:], a2_grouped[:])
+
+        due = {}
+        for name, lag in LAG.items():
+            for b in range(len(SIZES)):
+                at = FIRST[b] + lag[0] * SIZES[b] + lag[1]
+                if name in BLOCK_STAGES:
+                    due.setdefault((name, at), []).append((b,))
+                else:
+                    for j in range(SIZES[b]):
+                        due.setdefault((name, at + j), []).append((b, j))
+        steps = max([step for name, step in due.keys()]) + 1
+
+        def run(stage, name, step):
+            for unit in due.get((name, step), []):
+                stage(*unit)
+
+        def load_ahead(b):
+            if b + AHEAD < len(SIZES):
+                load(b + AHEAD)
 
         with tc.manual_schedule():
-            for step in range(-1, BLOCKS * TILES + O_STORE + 1):
-                for_tile(q_transpose, step + 1 - Q_COPY)
-                for_tile(y_transpose, step + 1 - J1_PLANE)
-                for_tile(u_matmul, step + 1 - U_BIAS)
-                for_tile(w_matmul, step + 1 - W_BIAS)
-
-                for_block(u_stats, step - U_STATS)
-                for_block(w_stats, step - W_STATS)
-                for_tile(u_offset, step - U_NORMALISE)
-                for_tile(u_normalise, step - U_NORMALISE)
-                for_tile(u_bias, step - U_BIAS)
-                for_tile(w_bias, step - W_BIAS)
-                for_tile(j1_quantise, step - J1_QUANTISE)
-                for_tile(w_gain, step - W_GAIN)
-                for_tile(q_quantise, step - Q_QUANTISE)
-                for_tile(w_shift, step - W_SHIFT)
-                for_block(u_rstd, step - U_RSTD)
-                for_block(w_rstd, step - W_RSTD)
-                for_tile(j1_group, step - J1_GROUP)
-                for_tile(q_copy, step - Q_COPY)
-                for_tile(j1_plane, step - J1_PLANE)
-                for_tile(u_squares, step - U_BIAS)
-                for_tile(w_squares, step - W_BIAS)
-                for_tile(o_relu, step - O_RELU)
-                for_block(o_store, step - O_STORE)
-                for_block(load, step - LOAD, ahead=3)
+            for step in range(-1, steps):
+                run(u_stats, "u_stats", step)
+                run(w_stats, "w_stats", step)
+                run(u_offset, "u_normalise", step)
+                run(u_normalise, "u_normalise", step)
+                run(j1_quantise, "j1_quantise", step)
+                run(u_bias, "u_bias", step)
+                run(w_bias, "w_bias", step)
+                run(w_gain, "w_gain", step)
+                run(j1_group, "j1_group", step)
+                run(q_quantise, "q_quantise", step)
+                run(w_shift, "w_shift", step)
+                run(q_copy, "q_copy", step)
+                run(j1_plane, "j1_plane", step)
+                run(u_squares, "u_bias", step)
+                run(w_squares, "w_bias", step)
+                run(o_relu, "o_relu", step)
+                if step == LATER_CONSTANTS:
+                    later_constants()
+                run(o_store, "o_store", step)
+                run(load_ahead, "load", step)
+                run(q_transpose, "q_copy", step + 1)
+                run(y_transpose, "j1_plane", step + 1)
+                run(u_matmul, "u_bias", step + 1)
+                run(w_matmul, "w_bias", step + 1)

@@ -36,15 +36,19 @@ LAG = {
     "j1_plane": (2, 5),
     "j1_group": (3, 5),
     "j1_quantise": (3, 6),
-    "w_bias": (3, 7),
-    "w_stats": (4, 7),
-    "w_gain": (4, 8),
-    "w_shift": (4, 9),
-    "o_relu": (4, 10),
-    "o_store": (5, 9),
+    "w_bias": (3, 8),
+    "w_stats": (4, 8),
+    "w_gain": (4, 9),
+    "w_shift": (4, 10),
+    "o_relu": (4, 11),
+    "o_store": (5, 10),
 }
 BLOCK_STAGES = ("load", "u_stats", "w_stats", "o_store")
-LATER_CONSTANTS = 5
+LATER_CONSTANTS = 7
+A2_GROUP = 10
+A2_QUANTISE = 12
+V_GROUPS = 3
+S_GROUPS = 13
 
 
 def group_weight(nc, grouped, raw, strands):
@@ -70,6 +74,7 @@ def tile_multiheadedattention_pa_t_kernel(tc, query, A1W, A1b, g1, b1, A2W, A2b,
         small = ctx.enter_context(tc.tile_pool(name="small", bufs=6))
         deep = ctx.enter_context(tc.tile_pool(name="deep", bufs=12))
         psum = ctx.enter_context(tc.psum_pool(name="psum", bufs=2))
+        psum_one = ctx.enter_context(tc.psum_pool(name="psum_one", bufs=1))
 
         held = {}
 
@@ -217,10 +222,21 @@ def tile_multiheadedattention_pa_t_kernel(tc, query, A1W, A1b, g1, b1, A2W, A2b,
 
         def j1_group(b, j):
             j1_grouped = three.tile([P, P, PACK], BF16, align_bytes=64, name="j1_grouped")
-            (nc.scalar.copy if (j == 3 and b % 2) or (j % 2 == 1 and b >= 13) else nc.vector.tensor_copy)(
-                out=j1_grouped[:].rearrange("p (c i) t -> p c t i", i=4),
-                in_=held["j1_planes", b][:, :, j * P : (j + 1) * P].rearrange("p t (c i) -> p c t i", i=4),
-            )
+            grouped = j1_grouped[:].rearrange("p (c i) t -> p c t i", i=4)
+            planes_of_tile = held["j1_planes", b][:, :, j * P : (j + 1) * P].rearrange("p t (c i) -> p c t i", i=4)
+            if b < V_GROUPS:
+                nc.vector.tensor_copy(out=grouped, in_=planes_of_tile)
+            elif b >= S_GROUPS and j % 2:
+                nc.scalar.copy(out=grouped, in_=planes_of_tile)
+            else:
+                nc.gpsimd.tensor_scalar(
+                    out=j1_grouped[:],
+                    in0=held["j1_planes", b][:, :, j * P : (j + 1) * P].rearrange("p t r -> p r t"),
+                    scalar1=1.0,
+                    scalar2=0.0,
+                    op0=ALU.mult,
+                    op1=ALU.add,
+                )
             held["j1_grouped", b, j] = j1_grouped
 
         def j1_quantise(b, j):
@@ -235,7 +251,7 @@ def tile_multiheadedattention_pa_t_kernel(tc, query, A1W, A1b, g1, b1, A2W, A2b,
             held["j1_scales", b, j] = j1_scales
 
         def w_matmul(b, j):
-            mm2 = psum.tile([P, D4], F32, name="mm2")
+            mm2 = psum_one.tile([P, D4], F32, name="mm2")
             nc.tensor.matmul_mx(
                 out=mm2[:],
                 lhsT=held["j1_codes", b, j][:].bitcast(FP8X4),
@@ -285,13 +301,8 @@ def tile_multiheadedattention_pa_t_kernel(tc, query, A1W, A1b, g1, b1, A2W, A2b,
                 scale=1.0 / (D4 * D4 * D4),
             )
             held["w_negmean", b] = small.tile([P, SIZES[b]], F32, name="w_negmean")
-            nc.gpsimd.tensor_scalar(
-                out=held["w_negmean", b][:],
-                in0=held["w_sum", b][:],
-                scalar1=-1.0 / D4,
-                scalar2=0.0,
-                op0=ALU.mult,
-                op1=ALU.add,
+            nc.scalar.activation(
+                out=held["w_negmean", b][:], in_=held["w_sum", b][:], func=ACT.Copy, scale=-1.0 / D4
             )
 
         def w_gain(b, j):
@@ -300,7 +311,7 @@ def tile_multiheadedattention_pa_t_kernel(tc, query, A1W, A1b, g1, b1, A2W, A2b,
                 out=w_gain_sb[:],
                 in0=held["w", b, j][:],
                 scalar=held["w_negmean", b][:, j : j + 1],
-                in1=g2_all[:],
+                in1=gb2[:, 0, :],
                 op0=ALU.add,
                 op1=ALU.mult,
             )
@@ -313,19 +324,30 @@ def tile_multiheadedattention_pa_t_kernel(tc, query, A1W, A1b, g1, b1, A2W, A2b,
                 out=held["o", b][:, j, :],
                 in0=held["w_gain", b, j][:],
                 scalar=held["w_rstd", b][:, j : j + 1],
-                in1=b2_all[:],
+                in1=gb2[:, 1, :],
                 op0=ALU.mult,
                 op1=ALU.add,
             )
 
         def o_relu(b, j):
             o_tile = held["o", b][:, j, :]
-            nc.scalar.activation(out=o_tile, in_=o_tile, func=ACT.Relu)
+            if j % 2 or b >= S_GROUPS:
+                nc.scalar.activation(out=o_tile, in_=o_tile, func=ACT.Relu)
+            else:
+                nc.vector.tensor_scalar_max(out=o_tile, in0=o_tile, scalar1=0.0)
 
         def o_store(b):
-            nc.sync.dma_start(
-                out=out_rows[block_rows(b), :].rearrange("(p j) n -> p j n", j=SIZES[b]), in_=held["o", b][:]
-            )
+            if b < len(SIZES) - 1:
+                nc.sync.dma_start(
+                    out=out_rows[block_rows(b), :].rearrange("(p j) n -> p j n", j=SIZES[b]), in_=held["o", b][:]
+                )
+
+        def o_store_tile(b, j):
+            if b == len(SIZES) - 1:
+                nc.sync.dma_start(
+                    out=out_rows[block_rows(b), :].rearrange("(p j) n -> p j n", j=SIZES[b])[:, j, :],
+                    in_=held["o", b][:, j, :],
+                )
 
         a1_raw = const.tile([P, PASSES, PACK, D2], BF16)
         for g in range(PASSES):
@@ -358,6 +380,8 @@ def tile_multiheadedattention_pa_t_kernel(tc, query, A1W, A1b, g1, b1, A2W, A2b,
         nc.scalar.activation(out=warm[:], in_=eps[:], func=ACT.Abs_reciprocal_sqrt)
         ident = const.tile([P, P], F32)
         make_identity(nc, ident[:])
+        ident_bf16 = const.tile([P, P], BF16)
+        nc.vector.tensor_copy(out=ident_bf16[:], in_=ident[:])
 
         a1_grouped = const.tile([P, PASSES, D2, PACK], BF16, align_bytes=64)
         a1_codes = const.tile([P, PASSES, D2], U32, align_bytes=64)
@@ -376,13 +400,20 @@ def tile_multiheadedattention_pa_t_kernel(tc, query, A1W, A1b, g1, b1, A2W, A2b,
         a2_codes = const.tile([P, D4], U32, align_bytes=64)
         a2_scales = const.tile([P, D4], U8, align_bytes=64)
         a2_grouped = const.tile([P, D4, PACK], BF16, align_bytes=64)
+        gb2 = psum_one.tile([P, 2, D4], F32, name="gb2")
 
         def later_constants():
             nc.vector.tensor_copy(out=gb_cols[:, 0:PACK], in_=g1_raw[:])
             nc.vector.tensor_copy(out=gb_cols[:, PACK : 2 * PACK], in_=b1_raw[:])
 
+        def a2_group():
             group_weight(nc, a2_grouped[:], a2_raw[:], 1)
+
+        def a2_quantise():
             quantise_weight(nc, a2_codes[:], a2_scales[:], a2_grouped[:])
+
+            for n, vector in enumerate((g2_all, b2_all)):
+                nc.tensor.matmul(gb2[:, n, :], lhsT=ident_bf16[:], rhs=vector[:], start=True, stop=True)
 
         due = {}
         for name, lag in LAG.items():
@@ -409,13 +440,13 @@ def tile_multiheadedattention_pa_t_kernel(tc, query, A1W, A1b, g1, b1, A2W, A2b,
                 run(w_stats, "w_stats", step)
                 run(u_offset, "u_normalise", step)
                 run(u_normalise, "u_normalise", step)
-                run(j1_quantise, "j1_quantise", step)
+                run(j1_group, "j1_group", step)
                 run(u_bias, "u_bias", step)
                 run(w_bias, "w_bias", step)
                 run(w_gain, "w_gain", step)
-                run(j1_group, "j1_group", step)
-                run(q_quantise, "q_quantise", step)
                 run(w_shift, "w_shift", step)
+                run(j1_quantise, "j1_quantise", step)
+                run(q_quantise, "q_quantise", step)
                 run(q_copy, "q_copy", step)
                 run(j1_plane, "j1_plane", step)
                 run(u_squares, "u_bias", step)
@@ -423,7 +454,12 @@ def tile_multiheadedattention_pa_t_kernel(tc, query, A1W, A1b, g1, b1, A2W, A2b,
                 run(o_relu, "o_relu", step)
                 if step == LATER_CONSTANTS:
                     later_constants()
+                if step == A2_GROUP:
+                    a2_group()
+                if step == A2_QUANTISE:
+                    a2_quantise()
                 run(o_store, "o_store", step)
+                run(o_store_tile, "o_relu", step)
                 run(load_ahead, "load", step)
                 run(q_transpose, "q_copy", step + 1)
                 run(y_transpose, "j1_plane", step + 1)

@@ -36,18 +36,19 @@ LAG = {
     "j1_plane": (2, 5),
     "j1_group": (3, 5),
     "j1_quantise": (3, 6),
-    "w_bias": (3, 8),
-    "w_stats": (4, 8),
-    "w_gain": (4, 9),
-    "w_shift": (4, 10),
-    "o_relu": (4, 11),
-    "o_store": (5, 10),
+    "w_bias": (3, 7),
+    "w_stats": (4, 7),
+    "w_gain": (4, 8),
+    "w_shift": (4, 9),
+    "o_relu": (4, 10),
+    "o_store": (5, 9),
 }
 BLOCK_STAGES = ("load", "u_stats", "w_stats", "o_store")
 LATER_CONSTANTS = 7
 A2_GROUP = 10
 A2_QUANTISE = 12
 V_GROUPS = 3
+G_ROWS = 64
 S_GROUPS = 13
 
 
@@ -222,21 +223,22 @@ def tile_multiheadedattention_pa_t_kernel(tc, query, A1W, A1b, g1, b1, A2W, A2b,
 
         def j1_group(b, j):
             j1_grouped = three.tile([P, P, PACK], BF16, align_bytes=64, name="j1_grouped")
-            grouped = j1_grouped[:].rearrange("p (c i) t -> p c t i", i=4)
-            planes_of_tile = held["j1_planes", b][:, :, j * P : (j + 1) * P].rearrange("p t (c i) -> p c t i", i=4)
-            if b < V_GROUPS:
-                nc.vector.tensor_copy(out=grouped, in_=planes_of_tile)
-            elif b >= S_GROUPS and j % 2:
-                nc.scalar.copy(out=grouped, in_=planes_of_tile)
-            else:
+            planes_of_tile = held["j1_planes", b][:, :, j * P : (j + 1) * P]
+            scalar_shares = b >= S_GROUPS and j % 2
+            g_rows = 0 if b < V_GROUPS or scalar_shares else G_ROWS
+            if g_rows:
                 nc.gpsimd.tensor_scalar(
-                    out=j1_grouped[:],
-                    in0=held["j1_planes", b][:, :, j * P : (j + 1) * P].rearrange("p t r -> p r t"),
+                    out=j1_grouped[:, :g_rows, :],
+                    in0=planes_of_tile[:, :, :g_rows].rearrange("p t r -> p r t"),
                     scalar1=1.0,
                     scalar2=0.0,
                     op0=ALU.mult,
                     op1=ALU.add,
                 )
+            (nc.scalar.copy if scalar_shares else nc.vector.tensor_copy)(
+                out=j1_grouped[:, g_rows:, :].rearrange("p (c i) t -> p c t i", i=4),
+                in_=planes_of_tile[:, :, g_rows:].rearrange("p t (c i) -> p c t i", i=4),
+            )
             held["j1_grouped", b, j] = j1_grouped
 
         def j1_quantise(b, j):
@@ -331,7 +333,7 @@ def tile_multiheadedattention_pa_t_kernel(tc, query, A1W, A1b, g1, b1, A2W, A2b,
 
         def o_relu(b, j):
             o_tile = held["o", b][:, j, :]
-            if j % 2 or b >= S_GROUPS:
+            if j != 1 or b >= S_GROUPS:
                 nc.scalar.activation(out=o_tile, in_=o_tile, func=ACT.Relu)
             else:
                 nc.vector.tensor_scalar_max(out=o_tile, in0=o_tile, scalar1=0.0)
@@ -440,12 +442,12 @@ def tile_multiheadedattention_pa_t_kernel(tc, query, A1W, A1b, g1, b1, A2W, A2b,
                 run(w_stats, "w_stats", step)
                 run(u_offset, "u_normalise", step)
                 run(u_normalise, "u_normalise", step)
-                run(j1_group, "j1_group", step)
+                run(j1_quantise, "j1_quantise", step)
                 run(u_bias, "u_bias", step)
                 run(w_bias, "w_bias", step)
                 run(w_gain, "w_gain", step)
                 run(w_shift, "w_shift", step)
-                run(j1_quantise, "j1_quantise", step)
+                run(j1_group, "j1_group", step)
                 run(q_quantise, "q_quantise", step)
                 run(q_copy, "q_copy", step)
                 run(j1_plane, "j1_plane", step)

@@ -21,7 +21,7 @@ EPS = 1e-5
 PASSES = D // (P * PACK)
 AHEAD = 3
 
-SIZES = [4] * 17
+SIZES = [2, 2] + [4] * 16
 FIRST = [sum(SIZES[:b]) for b in range(len(SIZES))]
 
 FLOPS = 2 * ROWS * (D * D2 + D2 * D4)
@@ -49,7 +49,7 @@ A2_GROUP = 10
 A2_QUANTISE = 12
 V_GROUPS = 3
 G_ROWS = 64
-S_GROUPS = 13
+S_GROUPS = 14
 
 
 def group_weight(nc, grouped, raw, strands):
@@ -463,7 +463,7 @@ def tile_multiheadedattention_pa_t_kernel(tc, query, A1W, A1b, g1, b1, A2W, A2b,
                 run(o_store, "o_store", step)
                 run(o_store_tile, "o_relu", step)
                 run(load_ahead, "load", step)
+                run(u_matmul, "u_bias", step + 1)
                 run(q_transpose, "q_copy", step + 1)
                 run(y_transpose, "j1_plane", step + 1)
-                run(u_matmul, "u_bias", step + 1)
                 run(w_matmul, "w_bias", step + 1)

from contextlib import ExitStack

import concourse.mybir as mybir
from concourse.masks import make_identity

F32 = mybir.dt.float32
BF16 = mybir.dt.bfloat16
U32 = mybir.dt.uint32
U8 = mybir.dt.uint8
FP8X4 = mybir.dt.float8_e4m3fn_x4
ALU = mybir.AluOpType
ACT = mybir.ActivationFunctionType

P = 128
PACK = 4
ROWS = 512 * 17
D = 1024
D2 = 512
D4 = 256
EPS = 1e-5
PASSES = D // (P * PACK)
AHEAD = 3

SIZES = [2, 2] + [4] * 16
FIRST = [sum(SIZES[:b]) for b in range(len(SIZES))]

FLOPS = 2 * ROWS * (D * D2 + D2 * D4)

LAG = {
    "load": (1, -1),
    "q_copy": (0, 0),
    "q_quantise": (0, 1),
    "u_bias": (0, 3),
    "u_stats": (1, 3),
    "u_normalise": (1, 4),
    "j1_plane": (2, 5),
    "j1_group": (3, 5),
    "j1_quantise": (3, 6),
    "w_bias": (3, 7),
    "w_stats": (4, 7),
    "w_gain": (4, 8),
    "w_shift": (4, 9),
    "o_relu": (4, 10),
    "o_store": (5, 9),
}
BLOCK_STAGES = ("load", "u_stats", "w_stats", "o_store")
LATER_CONSTANTS = 7
A2_GROUP = 10
A2_QUANTISE = 12
V_GROUPS = 3
G_ROWS = 64
S_GROUPS = 14


def group_weight(nc, grouped, raw, strands):
    nc.vector.tensor_copy(
        out=grouped.rearrange("p (s m) t -> p s m t", s=strands),
        in_=raw.rearrange("p t (m s) -> p s m t", s=strands),
    )


def quantise_weight(nc, codes, scales, grouped):
    nc.vector.quantize_mx(out=codes.bitcast(FP8X4), scales=scales, in_=grouped.rearrange("p n t -> p (n t)"))


def tile_multiheadedattention_pa_t_kernel(tc, query, A1W, A1b, g1, b1, A2W, A2b, g2, b2, out):
    nc = tc.nc
    q_rows = query.flatten_outer_dims()
    out_rows = out.flatten_outer_dims()

    with ExitStack() as ctx:
        const = ctx.enter_context(tc.tile_pool(name="const", bufs=1))
        two = ctx.enter_context(tc.tile_pool(name="two", bufs=2))
        three = ctx.enter_context(tc.tile_pool(name="three", bufs=3))
        small = ctx.enter_context(tc.tile_pool(name="small", bufs=6))
        deep = ctx.enter_context(tc.tile_pool(name="deep", bufs=12))
        psum = ctx.enter_context(tc.psum_pool(name="psum", bufs=2))
        psum_one = ctx.enter_context(tc.psum_pool(name="psum_one", bufs=1))

        held = {}

        def block_rows(b):
            return slice(FIRST[b] * P, (FIRST[b] + SIZES[b]) * P)

        def load(b):
            q_sb = three.tile([P, SIZES[b], D], BF16, name="q_sb")
            nc.sync.dma_start(out=q_sb[:], in_=q_rows[block_rows(b), :].rearrange("(p j) k -> p j k", j=SIZES[b]))
            held["q_sb", b] = q_sb

        def load_tile(b, j):
            if j == 0:
                held["q_sb", b] = three.tile([P, SIZES[b], D], BF16, name="q_sb")
            nc.sync.dma_start(
                out=held["q_sb", b][:, j, :],
                in_=q_rows[block_rows(b), :].rearrange("(p j) k -> p j k", j=SIZES[b])[:, j, :],
            )

        def q_transpose(b, j):
            q_words = held["q_sb", b][:, j, :].bitcast(F32)
            qT = psum.tile([P, PASSES, 2, P], F32, name="qT")
            for g in range(PASSES):
                for u in range(2):
                    col = g * 2 * P + u
                    nc.tensor.transpose(qT[:, g, u, :], q_words[:, col : col + 2 * P - 1 : 2], ident[:])
            held["qT", b, j] = qT

        def q_copy(b, j):
            qg = three.tile([P, D], BF16, align_bytes=64, name="qg")
            nc.scalar.copy(
                out=qg[:].bitcast(F32).rearrange("p (g r u) -> p g r u", g=PASSES, u=2),
                in_=held["qT", b, j][:].rearrange("p g u r -> p g r u"),
            )
            held["qg", b, j] = qg

        def q_quantise(b, j):
            q_codes = three.tile([P, PASSES * P], U32, align_bytes=64, name="q_codes")
            q_scales = three.tile([P, PASSES * P], U8, align_bytes=64, name="q_scales")
            nc.vector.quantize_mx(out=q_codes[:].bitcast(FP8X4), scales=q_scales[:], in_=held["qg", b, j][:])
            held["q_codes", b, j] = q_codes
            held["q_scales", b, j] = q_scales

        def u_matmul(b, j):
            mm1 = psum.tile([P, D2], F32, name="mm1")
            for g in range(PASSES):
                cols = slice(g * P, (g + 1) * P)
                nc.tensor.matmul_mx(
                    out=mm1[:],
                    lhsT=held["q_codes", b, j][:, cols].bitcast(FP8X4),
                    lhsT_scale=held["q_scales", b, j][:, cols],
                    rhs=a1_codes[:, g, :].bitcast(FP8X4),
                    rhs_scale=a1_scales[:, g, :],
                    start=(g == 0),
                    stop=(g == PASSES - 1),
                )
            held["mm1", b, j] = mm1

        def u_bias(b, j):
            if j == 0:
                held["u_sum", b] = small.tile([P, SIZES[b]], F32, name="u_sum")
            u_sb = deep.tile([P, D2], F32, name="u_sb")
            nc.vector.scalar_tensor_tensor(
                out=u_sb[:],
                in0=held["mm1", b, j][:],
                scalar=1.0,
                in1=a1b_all[:],
                op0=ALU.mult,
                op1=ALU.add,
                accum_out=held["u_sum", b][:, j : j + 1],
            )
            held["u", b, j] = u_sb

        def u_squares(b, j):
            if j == 0:
                held["u_ssq", b] = small.tile([P, SIZES[b]], F32, name="u_ssq")
            u_sq = two.tile([P, D2], BF16, name="u_sq")
            nc.scalar.activation(
                out=u_sq[:],
                in_=held["u", b, j][:],
                func=ACT.Square,
                bias=held["u_sum", b][:, j : j + 1],
                scale=-1.0 * D2,
                accum_out=held["u_ssq", b][:, j : j + 1],
            )

        def u_stats(b):
            held["u_rstd", b] = small.tile([P, SIZES[b]], F32, name="u_rstd")
            nc.scalar.activation(
                out=held["u_rstd", b][:],
                in_=held["u_ssq", b][:],
                func=ACT.Abs_reciprocal_sqrt,
                bias=eps[:, 0:1],
                scale=1.0 / (D2 * D2 * D2),
            )

        def u_offset(b, j):
            if j == 0:
                held["u_offset", b] = small.tile([P, SIZES[b]], F32, name="u_offset")
            nc.vector.scalar_tensor_tensor(
                out=held["u_offset", b][:, j : j + 1],
                in0=held["u_sum", b][:, j : j + 1],
                scalar=-1.0 / D2,
                in1=held["u_rstd", b][:, j : j + 1],
                op0=ALU.mult,
                op1=ALU.mult,
            )

        def u_normalise(b, j):
            y_sb = deep.tile([P, D2], F32, name="y_sb")
            nc.gpsimd.tensor_scalar(
                out=y_sb[:],
                in0=held["u", b, j][:],
                scalar1=held["u_rstd", b][:, j : j + 1],
                scalar2=held["u_offset", b][:, j : j + 1],
                op0=ALU.mult,
                op1=ALU.add,
            )
            held["y", b, j] = y_sb

        def planes(b, i):
            turn = PACK // SIZES[b]
            return range(i * turn, (i + 1) * turn)

        def y_transpose(b, i):
            yT = psum.tile([P, D2], F32, name="yT")
            for n, t in enumerate(planes(b, i)):
                for j in range(SIZES[b]):
                    at = (n * SIZES[b] + j) * P
                    nc.tensor.transpose(yT[:, at : at + P], held["y", b, j][:, t * P : (t + 1) * P], ident[:])
            held["yT", b, i] = yT

        def j1_plane(b, i):
            width = SIZES[b] * P
            if i == 0:
                held["j1_planes", b] = three.tile([P, PACK, width], BF16, name="j1_planes")
            for n, t in enumerate(planes(b, i)):
                nc.scalar.activation(
                    out=held["j1_planes", b][:, t, :],
                    in_=held["yT", b, i][:, n * width : (n + 1) * width],
                    func=ACT.Relu,
                    bias=gb_cols[:, PACK + t : PACK + t + 1],
                    scale=gb_cols[:, t : t + 1],
                )

        def j1_group(b, j):
            j1_grouped = three.tile([P, P, PACK], BF16, align_bytes=64, name="j1_grouped")
            planes_of_tile = held["j1_planes", b][:, :, j * P : (j + 1) * P]
            scalar_shares = b >= S_GROUPS and j % 2
            g_rows = 0 if b < V_GROUPS or scalar_shares else G_ROWS
            if g_rows:
                nc.gpsimd.tensor_scalar(
                    out=j1_grouped[:, :g_rows, :],
                    in0=planes_of_tile[:, :, :g_rows].rearrange("p t r -> p r t"),
                    scalar1=1.0,
                    scalar2=0.0,
                    op0=ALU.mult,
                    op1=ALU.add,
                )
            (nc.scalar.copy if scalar_shares else nc.vector.tensor_copy)(
                out=j1_grouped[:, g_rows:, :].rearrange("p (c i) t -> p c t i", i=4),
                in_=planes_of_tile[:, :, g_rows:].rearrange("p t (c i) -> p c t i", i=4),
            )
            held["j1_grouped", b, j] = j1_grouped

        def j1_quantise(b, j):
            j1_codes = three.tile([P, P], U32, align_bytes=64, name="j1_codes")
            j1_scales = three.tile([P, P], U8, align_bytes=64, name="j1_scales")
            nc.vector.quantize_mx(
                out=j1_codes[:].bitcast(FP8X4),
                scales=j1_scales[:],
                in_=held["j1_grouped", b, j][:].rearrange("p r t -> p (r t)"),
            )
            held["j1_codes", b, j] = j1_codes
            held["j1_scales", b, j] = j1_scales

        def w_matmul(b, j):
            mm2 = psum_one.tile([P, D4], F32, name="mm2")
            nc.tensor.matmul_mx(
                out=mm2[:],
                lhsT=held["j1_codes", b, j][:].bitcast(FP8X4),
                lhsT_scale=held["j1_scales", b, j][:],
                rhs=a2_codes[:].bitcast(FP8X4),
                rhs_scale=a2_scales[:],
                start=True,
                stop=True,
            )
            held["mm2", b, j] = mm2

        def w_bias(b, j):
            if j == 0:
                held["w_sum", b] = small.tile([P, SIZES[b]], F32, name="w_sum")
            w_sb = deep.tile([P, D4], F32, name="w_sb")
            nc.vector.scalar_tensor_tensor(
                out=w_sb[:],
                in0=held["mm2", b, j][:],
                scalar=1.0,
                in1=a2b_all[:],
                op0=ALU.mult,
                op1=ALU.add,
                accum_out=held["w_sum", b][:, j : j + 1],
            )
            held["w", b, j] = w_sb

        def w_squares(b, j):
            if j == 0:
                held["w_ssq", b] = small.tile([P, SIZES[b]], F32, name="w_ssq")
            w_sq = two.tile([P, D4], BF16, name="w_sq")
            nc.scalar.activation(
                out=w_sq[:],
                in_=held["w", b, j][:],
                func=ACT.Square,
                bias=held["w_sum", b][:, j : j + 1],
                scale=-1.0 * D4,
                accum_out=held["w_ssq", b][:, j : j + 1],
            )

        def w_stats(b):
            held["w_rstd", b] = small.tile([P, SIZES[b]], F32, name="w_rstd")
            nc.scalar.activation(
                out=held["w_rstd", b][:],
                in_=held["w_ssq", b][:],
                func=ACT.Abs_reciprocal_sqrt,
                bias=eps[:, 0:1],
                scale=1.0 / (D4 * D4 * D4),
            )
            held["w_negmean", b] = small.tile([P, SIZES[b]], F32, name="w_negmean")
            nc.scalar.activation(
                out=held["w_negmean", b][:], in_=held["w_sum", b][:], func=ACT.Copy, scale=-1.0 / D4
            )

        def w_gain(b, j):
            w_gain_sb = three.tile([P, D4], F32, name="w_gain_sb")
            nc.vector.scalar_tensor_tensor(
                out=w_gain_sb[:],
                in0=held["w", b, j][:],
                scalar=held["w_negmean", b][:, j : j + 1],
                in1=gb2[:, 0, :],
                op0=ALU.add,
                op1=ALU.mult,
            )
            held["w_gain", b, j] = w_gain_sb

        def w_shift(b, j):
            if j == 0:
                held["o", b] = three.tile([P, SIZES[b], D4], F32, name="o_sb")
            nc.vector.scalar_tensor_tensor(
                out=held["o", b][:, j, :],
                in0=held["w_gain", b, j][:],
                scalar=held["w_rstd", b][:, j : j + 1],
                in1=gb2[:, 1, :],
                op0=ALU.mult,
                op1=ALU.add,
            )

        def o_relu(b, j):
            o_tile = held["o", b][:, j, :]
            if j != 1 or b >= S_GROUPS:
                nc.scalar.activation(out=o_tile, in_=o_tile, func=ACT.Relu)
            else:
                nc.vector.tensor_scalar_max(out=o_tile, in0=o_tile, scalar1=0.0)

        def o_store(b):
            if b < len(SIZES) - 1:
                nc.sync.dma_start(
                    out=out_rows[block_rows(b), :].rearrange("(p j) n -> p j n", j=SIZES[b]), in_=held["o", b][:]
                )

        def o_store_tile(b, j):
            if b == len(SIZES) - 1:
                nc.sync.dma_start(
                    out=out_rows[block_rows(b), :].rearrange("(p j) n -> p j n", j=SIZES[b])[:, j, :],
                    in_=held["o", b][:, j, :],
                )

        a1_raw = const.tile([P, PASSES, PACK, D2], BF16)
        for g in range(PASSES):
            nc.sync.dma_start(
                out=a1_raw[:, g, :, :],
                in_=A1W[g * P * PACK : (g + 1) * P * PACK, :].rearrange("(p t) n -> p t n", t=PACK),
            )
        for j in range(SIZES[0]):
            load_tile(0, j)
        a1b_raw = const.tile([P, D2], BF16)
        nc.sync.dma_start(out=a1b_raw[:], in_=A1b.partition_broadcast(P))
        load(1)
        g1_raw = const.tile([P, PACK], BF16)
        nc.sync.dma_start(out=g1_raw[:], in_=g1.rearrange("(p t) -> p t", t=PACK))
        b1_raw = const.tile([P, PACK], BF16)
        nc.sync.dma_start(out=b1_raw[:], in_=b1.rearrange("(p t) -> p t", t=PACK))
        a2_raw = const.tile([P, PACK, D4], BF16)
        nc.sync.dma_start(out=a2_raw[:], in_=A2W.rearrange("(p t) n -> p t n", t=PACK))
        load(2)
        a2b_all = const.tile([P, D4], BF16)
        nc.sync.dma_start(out=a2b_all[:], in_=A2b.partition_broadcast(P))
        g2_all = const.tile([P, D4], BF16)
        nc.sync.dma_start(out=g2_all[:], in_=g2.partition_broadcast(P))
        b2_all = const.tile([P, D4], BF16)
        nc.sync.dma_start(out=b2_all[:], in_=b2.partition_broadcast(P))

        eps = const.tile([P, 1], F32)
        nc.vector.memset(eps[:], EPS)
        warm = const.tile([P, 1], F32)
        nc.scalar.activation(out=warm[:], in_=eps[:], func=ACT.Abs_reciprocal_sqrt)
        ident = const.tile([P, P], F32)
        make_identity(nc, ident[:])
        ident_bf16 = const.tile([P, P], BF16)
        nc.vector.tensor_copy(out=ident_bf16[:], in_=ident[:])

        a1_grouped = const.tile([P, PASSES, D2, PACK], BF16, align_bytes=64)
        a1_codes = const.tile([P, PASSES, D2], U32, align_bytes=64)
        a1_scales = const.tile([P, PASSES, D2], U8, align_bytes=64)
        for g in range(PASSES):
            group_weight(nc, a1_grouped[:, g, :, :], a1_raw[:, g, :, :], PACK)
        for g in range(PASSES):
            quantise_weight(nc, a1_codes[:, g, :], a1_scales[:, g, :], a1_grouped[:, g, :, :])

        a1b_all = const.tile([P, D2], BF16)
        nc.vector.tensor_copy(
            out=a1b_all[:].rearrange("p (s m) -> p s m", s=PACK), in_=a1b_raw[:].rearrange("p (m s) -> p s m", s=PACK)
        )

        gb_cols = const.tile([P, 2 * PACK], F32)
        a2_codes = const.tile([P, D4], U32, align_bytes=64)
        a2_scales = const.tile([P, D4], U8, align_bytes=64)
        a2_grouped = const.tile([P, D4, PACK], BF16, align_bytes=64)
        gb2 = psum_one.tile([P, 2, D4], F32, name="gb2")

        def later_constants():
            nc.vector.tensor_copy(out=gb_cols[:, 0:PACK], in_=g1_raw[:])
            nc.vector.tensor_copy(out=gb_cols[:, PACK : 2 * PACK], in_=b1_raw[:])

        def a2_group():
            group_weight(nc, a2_grouped[:], a2_raw[:], 1)

        def a2_quantise():
            quantise_weight(nc, a2_codes[:], a2_scales[:], a2_grouped[:])

            for n, vector in enumerate((g2_all, b2_all)):
                nc.tensor.matmul(gb2[:, n, :], lhsT=ident_bf16[:], rhs=vector[:], start=True, stop=True)

        due = {}
        for name, lag in LAG.items():
            for b in range(len(SIZES)):
                at = FIRST[b] + lag[0] * SIZES[b] + lag[1]
                if name in BLOCK_STAGES:
                    due.setdefault((name, at), []).append((b,))
                else:
                    for j in range(SIZES[b]):
                        due.setdefault((name, at + j), []).append((b, j))
        steps = max([step for name, step in due.keys()]) + 1

        def run(stage, name, step):
            for unit in due.get((name, step), []):
                stage(*unit)

        def load_ahead(b):
            if b + AHEAD < len(SIZES):
                load(b + AHEAD)

        with tc.manual_schedule():
            for step in range(-1, steps):
                run(u_stats, "u_stats", step)
                run(w_stats, "w_stats", step)
                run(u_offset, "u_normalise", step)
                run(u_normalise, "u_normalise", step)
                run(j1_quantise, "j1_quantise", step)
                run(u_bias, "u_bias", step)
                run(w_bias, "w_bias", step)
                run(w_gain, "w_gain", step)
                run(w_shift, "w_shift", step)
                run(j1_group, "j1_group", step)
                run(q_quantise, "q_quantise", step)
                run(q_copy, "q_copy", step)
                run(j1_plane, "j1_plane", step)
                run(u_squares, "u_bias", step)
                run(w_squares, "w_bias", step)
                run(o_relu, "o_relu", step)
                if step == LATER_CONSTANTS:
                    later_constants()
                if step == A2_GROUP:
                    a2_group()
                if step == A2_QUANTISE:
                    a2_quantise()
                run(o_store, "o_store", step)
                run(o_store_tile, "o_relu", step)
                run(load_ahead, "load", step)
                run(u_matmul, "u_bias", step + 1)
                run(q_transpose, "q_copy", step + 1)
                run(y_transpose, "j1_plane", step + 1)
                run(w_matmul, "w_bias", step + 1)
